import numpy as np
import ml_dtypes


def mxq(x, axis, fmt="e4m3"):
    dtype, down = {"e4m3": (ml_dtypes.float8_e4m3fn, 7), "e5m2": (ml_dtypes.float8_e5m2, 14)}[fmt]
    v = np.moveaxis(np.asarray(x, np.float32).astype(ml_dtypes.bfloat16).astype(np.float64), axis, -1)
    blocks = v.reshape(v.shape[:-1] + (-1, 32))
    amax = np.abs(blocks).max(-1, keepdims=True)
    byte = np.maximum(np.where(amax > 0, np.frexp(amax)[1] - 1 + 127, 0) - down, 1)
    scale = np.exp2(byte - 127.0)
    codes = (blocks / scale).astype(np.float32).astype(dtype).astype(np.float64)
    return np.moveaxis((codes * scale).reshape(v.shape), -1, axis)


WIDE = False


def mx_kscale(k):
    if not WIDE:
        return np.ones(k)
    levels = np.array([10, -10, 5, -5, 0])
    if k % 512:
        return np.exp2(np.random.permutation(np.resize(levels, k // 32))).repeat(32)
    a = np.empty((k // 512, 16))
    for p in range(k // 512):
        a[p, :8] = np.random.permutation(np.resize(levels, 8))
        for g in range(8):
            far = levels[np.abs(levels - a[p, g]) >= 10]
            a[p, g + 8] = far[np.random.randint(len(far))]
    return np.exp2(a.ravel()).repeat(32)


BF16 = ml_dtypes.bfloat16


def bf(x):
    return np.asarray(x, np.float32).astype(BF16)


def f64(x):
    return np.asarray(x).astype(np.float64)


B, C_IN, H, W, N_HID, N_CLS = 1024, 3, 32, 32, 1024, 128
D = C_IN * H * W
EPS = 1e-12
BN_EPS = 1e-5


def unit_rows(v):
    return v / (np.sqrt((v * v).sum(axis=1, keepdims=True)) + EPS)


def batchnorm(c, gamma, beta):
    mu = c.mean(axis=0)
    var = c.var(axis=0)
    return (c - mu) * (1.0 / np.sqrt(var + BN_EPS)) * gamma + beta


def setup_inputs():
    s = mx_kscale(D)
    r = np.sqrt(np.mean(s * s) * np.mean(1.0 / (s * s)))
    v = (0.5 - 0.5 / np.pi) / D
    comp = np.exp2(np.round(np.log2(r * np.sqrt((v / (r * r) + BN_EPS) / (v + BN_EPS)))))
    contrast = np.exp2(np.random.uniform(-1.0, 1.0, B))[:, None, None, None]
    length = np.exp2(np.random.uniform(-3.0, 0.0, N_HID))[:, None]
    return {"x": bf(np.random.standard_normal((B, C_IN, H, W)) * contrast * s.reshape(C_IN, H, W)),
            "w1": bf(np.random.standard_normal((N_HID, D)) * length / np.sqrt(D) / s[None, :]),
            "g1": bf((1.0 + 0.1 * np.random.standard_normal(N_HID)) * comp),
            "b1": bf(0.1 * np.random.standard_normal(N_HID))}


def reference(x, w1, g1, b1):
    xf = f64(x).reshape(B, -1)
    xn = unit_rows(xf)
    wn = unit_rows(f64(w1))
    c = np.clip(mxq(xn, 1, "e4m3") @ mxq(wn, 1, "e4m3").T, 0.0, 1.0)
    return batchnorm(c, f64(g1), f64(b1))

@@ -1,0 +1,298 @@
+from contextlib import ExitStack
+
+import concourse.masks as masks
+import concourse.mybir as mybir
+
+F32 = mybir.dt.float32
+BF16 = mybir.dt.bfloat16
+U32 = mybir.dt.uint32
+U8 = mybir.dt.uint8
+FP8X4 = mybir.dt.float8_e4m3fn_x4
+ALU = mybir.AluOpType
+ACT = mybir.ActivationFunctionType
+
+P = 128
+PACK = 4
+K_PASS = P * PACK
+BATCH = 1024
+HIDDEN = 1024
+DEPTH = 3072
+PASSES = DEPTH // K_PASS
+X_TILES = BATCH // P
+W_TILES = HIDDEN // P
+ROW_TILES = X_TILES + W_TILES
+PER_BANK = 4
+BANKS = DEPTH // 2 // (P * PER_BANK)
+N_MOVE = 512
+HALVES = BATCH // N_MOVE
+EPS = 1e-12
+BN_EPS = 1e-5
+LOADS_AHEAD = 6
+FIRST_SHARED = X_TILES + 2
+
+FLOPS = 2 * BATCH * HIDDEN * DEPTH
+
+
+def tile_net_pa_kernel(tc, x, w1, g1, b1, out):
+    nc = tc.nc
+    x_tiles = x.rearrange("(i p) c h w -> i p (c h w)", p=P)
+    w_tiles = w1.rearrange("(i p) k -> i p k", p=P)
+    rows_in_dram = [x_tiles[i] for i in range(X_TILES)] + [w_tiles[j] for j in range(W_TILES)]
+    out_tiles = out.rearrange("(t p) (j n) -> j p t n", p=P, n=P)
+
+    with ExitStack() as ctx:
+        const = ctx.enter_context(tc.tile_pool(name="const", bufs=1))
+        raw_pool = ctx.enter_context(tc.tile_pool(name="raw", bufs=LOADS_AHEAD + 2))
+        squares_pool = ctx.enter_context(tc.tile_pool(name="squares", bufs=2))
+        unit_pool = ctx.enter_context(tc.tile_pool(name="unit", bufs=3))
+        grouped_pool = ctx.enter_context(tc.tile_pool(name="grouped", bufs=3))
+        weight_pool = ctx.enter_context(tc.tile_pool(name="weight", bufs=3))
+        small = ctx.enter_context(tc.tile_pool(name="small", bufs=4))
+        sim_pool = ctx.enter_context(tc.tile_pool(name="sim", bufs=3))
+        normed_pool = ctx.enter_context(tc.tile_pool(name="normed", bufs=2))
+        result_pool = ctx.enter_context(tc.tile_pool(name="result", bufs=6))
+        turn_in_pool = ctx.enter_context(tc.psum_pool(name="turn_in", bufs=4))
+        turn_out_pool = ctx.enter_context(tc.psum_pool(name="turn_out", bufs=2))
+        acc_pool = ctx.enter_context(tc.psum_pool(name="acc", bufs=2))
+        ctx.enter_context(tc.manual_schedule())
+
+        power_half = const.tile([P, 1], F32)
+        nc.vector.memset(power_half[:], 0.5)
+        power_minus_half = const.tile([P, 1], F32)
+        nc.vector.memset(power_minus_half[:], -0.5)
+        power_minus_one = const.tile([P, 1], F32)
+        nc.vector.memset(power_minus_one[:], -1.0)
+
+        ident_f32 = const.tile([P, P], F32)
+        nc.vector.memset(ident_f32[:], 0.0)
+        masks.make_identity(nc, ident_f32[:], nomemset=True)
+
+        x_codes = const.tile([P, PASSES, BATCH], U32, align_bytes=64)
+        x_scales = const.tile([P, PASSES, BATCH], U8, align_bytes=64)
+
+        raw, norm, unit, turned_in, grouped = {}, {}, {}, {}, {}
+        weights, sums, sims, counts, lines, normeds, turned_out = {}, {}, {}, {}, {}, {}, {}
+
+        vector_rows = const.tile([P, P], BF16)
+        gain_shift = const.tile([P, 2 * W_TILES], F32)
+
+        def load_gain_and_shift():
+            nc.vector.memset(vector_rows[:], 0.0)
+            nc.sync.dma_start(out=vector_rows[0:W_TILES, :], in_=g1.rearrange("(j n) -> j n", n=P))
+            nc.sync.dma_start(
+                out=vector_rows[W_TILES : 2 * W_TILES, :], in_=b1.rearrange("(j n) -> j n", n=P)
+            )
+
+        def spread_gain_and_shift():
+            ident_bf16 = const.tile([P, P], BF16)
+            nc.vector.tensor_copy(out=ident_bf16[:], in_=ident_f32[:])
+            vector_cols = turn_out_pool.tile([P, P], BF16, tag="turned_back")
+            nc.tensor.transpose(vector_cols[:], vector_rows[:], ident_bf16[:])
+            nc.vector.tensor_copy(out=gain_shift[:, 0:W_TILES], in_=vector_cols[:, 0:W_TILES])
+            nc.vector.tensor_scalar_mul(
+                out=gain_shift[:, W_TILES : 2 * W_TILES],
+                in0=vector_cols[:, W_TILES : 2 * W_TILES],
+                scalar1=-1.0,
+            )
+
+        def load(r):
+            rows = raw_pool.tile([P, DEPTH], BF16)
+            nc.sync.dma_start(out=rows[:], in_=rows_in_dram[r])
+            raw[r] = rows
+
+        def measure(r):
+            squares = squares_pool.tile([P, DEPTH], BF16)
+            sum_squares = small.tile([P, 1], F32)
+            nc.scalar.activation(
+                out=squares[:], in_=raw[r][:], func=ACT.Square, accum_out=sum_squares[:]
+            )
+            length = small.tile([P, 1], F32)
+            nc.gpsimd.tensor_tensor(out=length[:], in0=sum_squares[:], in1=power_half[:], op=ALU.pow)
+            padded = small.tile([P, 1], F32)
+            nc.gpsimd.tensor_scalar(
+                out=padded[:], in0=length[:], scalar1=EPS, scalar2=1.0, op0=ALU.add, op1=ALU.mult
+            )
+            inverse = small.tile([P, 1], F32)
+            nc.gpsimd.tensor_tensor(
+                out=inverse[:], in0=padded[:], in1=power_minus_one[:], op=ALU.pow
+            )
+            norm[r] = inverse
+
+        def scale(r):
+            scaled = unit_pool.tile([P, DEPTH], BF16)
+            nc.vector.tensor_scalar_mul(out=scaled[:], in0=raw[r][:], scalar1=norm[r][:, 0:1])
+            unit[r] = scaled
+
+        def turn(r):
+            pairs = unit[r][:].bitcast(F32)
+            turned_in[r] = []
+            for m in range(BANKS):
+                turned = turn_in_pool.tile([P, PER_BANK, P], F32)
+                for q in range(PER_BANK):
+                    g, u = divmod(PER_BANK * m + q, 2)
+                    words = slice(2 * P * g + u, 2 * P * (g + 1), 2)
+                    nc.tensor.transpose(turned[:, q, :], pairs[:, words], ident_f32[:])
+                turned_in[r].append(turned)
+
+        def regroup(r):
+            lined = grouped_pool.tile([P, DEPTH], BF16, align_bytes=64)
+            lined_pairs = lined[:].bitcast(F32).rearrange("p (g c u) -> p g c u", g=PASSES, u=2)
+            for m in range(BANKS):
+                source = turned_in[r][m][:].rearrange("p (g u) c -> p g c u", u=2)
+                target = lined_pairs[:, 2 * m : 2 * m + 2, :, :]
+                if r >= FIRST_SHARED and m > 0:
+                    nc.scalar.copy(out=target, in_=source)
+                else:
+                    nc.vector.tensor_copy(out=target, in_=source)
+            grouped[r] = lined
+
+        def quantise(r):
+            if r < X_TILES:
+                cols = slice(r * P, (r + 1) * P)
+                for g in range(PASSES):
+                    nc.vector.quantize_mx(
+                        out=x_codes[:, g, cols].bitcast(FP8X4),
+                        scales=x_scales[:, g, cols],
+                        in_=grouped[r][:, g * K_PASS : (g + 1) * K_PASS],
+                    )
+            else:
+                w_codes = weight_pool.tile([P, PASSES * P], U32, align_bytes=64)
+                w_scales = weight_pool.tile([P, PASSES * P], U8, align_bytes=64)
+                for first, width in ((0, 4 * P), (4 * P, 2 * P)):
+                    nc.vector.quantize_mx(
+                        out=w_codes[:, first : first + width].bitcast(FP8X4),
+                        scales=w_scales[:, first : first + width],
+                        in_=grouped[r][:, PACK * first : PACK * (first + width)],
+                    )
+                weights[r - X_TILES] = (w_codes, w_scales)
+
+        def multiply(j):
+            w_codes, w_scales = weights[j]
+            sums[j] = []
+            for h in range(HALVES):
+                half = slice(h * N_MOVE, (h + 1) * N_MOVE)
+                acc = acc_pool.tile([P, N_MOVE], F32)
+                for g in range(PASSES):
+                    w_cols = slice(g * P, (g + 1) * P)
+                    nc.tensor.matmul_mx(
+                        out=acc[:],
+                        lhsT=w_codes[:, w_cols].bitcast(FP8X4),
+                        lhsT_scale=w_scales[:, w_cols],
+                        rhs=x_codes[:, g, half].bitcast(FP8X4),
+                        rhs_scale=x_scales[:, g, half],
+                        start=(g == 0),
+                        stop=(g == PASSES - 1),
+                    )
+                sums[j].append(acc)
+
+        def clip(j, h):
+            if h == 0:
+                sim = sim_pool.tile([P, BATCH], F32)
+                sims[j] = sim
+            half_cols = slice(h * N_MOVE, (h + 1) * N_MOVE)
+            nc.vector.tensor_scalar(
+                out=sims[j][:, half_cols], in0=sums[j][h][:], scalar1=0.0, scalar2=1.0,
+                op0=ALU.max, op1=ALU.min,
+            )
+
+        def count(j, h):
+            if h == 0:
+                stats = small.tile([P, HALVES, 6], F32)
+                counts[j] = stats
+            nc.vector.bn_stats(
+                out=counts[j][:, h, :], in_=sims[j][:, h * N_MOVE : (h + 1) * N_MOVE]
+            )
+
+        def fit(j):
+            mean_var = small.tile([P, 2], F32)
+            nc.vector.bn_aggr(out=mean_var[:], in_=counts[j][:].rearrange("p h s -> p (h s)"))
+            padded_var = small.tile([P, 1], F32)
+            nc.gpsimd.tensor_scalar(
+                out=padded_var[:], in0=mean_var[:, 1:2], scalar1=BN_EPS, scalar2=1.0,
+                op0=ALU.add, op1=ALU.mult,
+            )
+            inverse_std = small.tile([P, 1], F32)
+            nc.gpsimd.tensor_tensor(
+                out=inverse_std[:], in0=padded_var[:], in1=power_minus_half[:], op=ALU.pow
+            )
+            slope = small.tile([P, 1], F32)
+            nc.gpsimd.tensor_tensor(
+                out=slope[:], in0=inverse_std[:], in1=gain_shift[:, j : j + 1], op=ALU.mult
+            )
+            drop = small.tile([P, 1], F32)
+            nc.gpsimd.tensor_scalar(
+                out=drop[:], in0=mean_var[:, 0:1], scalar1=slope[:, 0:1],
+                scalar2=gain_shift[:, W_TILES + j : W_TILES + j + 1],
+                op0=ALU.mult, op1=ALU.add,
+            )
+            lines[j] = (slope, drop)
+
+        def normalise(j):
+            slope, drop = lines[j]
+            normed = normed_pool.tile([P, BATCH], F32)
+            for h in range(HALVES):
+                half_cols = slice(h * N_MOVE, (h + 1) * N_MOVE)
+                nc.vector.tensor_scalar(
+                    out=normed[:, half_cols], in0=sims[j][:, half_cols],
+                    scalar1=slope[:, 0:1], scalar2=drop[:, 0:1],
+                    op0=ALU.mult, op1=ALU.subtract,
+                )
+            normeds[j] = normed
+
+        def turn_back(j):
+            turned_out[j] = []
+            for m in range(X_TILES // PER_BANK):
+                turned_back = turn_out_pool.tile([P, PER_BANK, P], F32)
+                for q in range(PER_BANK):
+                    t = PER_BANK * m + q
+                    nc.tensor.transpose(
+                        turned_back[:, q, :], normeds[j][:, t * P : (t + 1) * P], ident_f32[:]
+                    )
+                turned_out[j].append(turned_back)
+
+        def store(j):
+            for m in range(X_TILES // PER_BANK):
+                result = result_pool.tile([P, PER_BANK, P], F32)
+                nc.scalar.copy(out=result[:], in_=turned_out[j][m][:])
+                nc.sync.dma_start(
+                    out=out_tiles[j][:, PER_BANK * m : PER_BANK * (m + 1), :], in_=result[:]
+                )
+
+        for r in range(LOADS_AHEAD):
+            load(r)
+        load_gain_and_shift()
+        for step in range(ROW_TILES + 6):
+            scaled_now = step - 1
+            grouped_now = step - 2
+            multiplied_now = step - 3 - X_TILES
+            fitted_now = step - 4 - X_TILES
+            stored_now = step - 5 - X_TILES
+            if 0 <= multiplied_now < W_TILES:
+                multiply(multiplied_now)
+            if 0 <= fitted_now < W_TILES:
+                count(fitted_now, 1)
+            if 0 <= grouped_now < ROW_TILES:
+                regroup(grouped_now)
+            if 0 <= fitted_now < W_TILES:
+                fit(fitted_now)
+            if step < ROW_TILES:
+                measure(step)
+            if 0 <= stored_now < W_TILES:
+                normalise(stored_now)
+                turn_back(stored_now)
+            if 0 <= scaled_now < ROW_TILES:
+                scale(scaled_now)
+                turn(scaled_now)
+            if 0 <= multiplied_now < W_TILES:
+                clip(multiplied_now, 0)
+            if 0 <= grouped_now < ROW_TILES:
+                quantise(grouped_now)
+            if 0 <= multiplied_now < W_TILES:
+                clip(multiplied_now, 1)
+                count(multiplied_now, 0)
+            if 0 <= stored_now < W_TILES:
+                store(stored_now)
+            if step + LOADS_AHEAD < ROW_TILES:
+                load(step + LOADS_AHEAD)
+            if step == X_TILES:
+                spread_gain_and_shift()

@@ -28,7 +28,18 @@ HALVES = BATCH // N_MOVE
 EPS = 1e-12
 BN_EPS = 1e-5
 LOADS_AHEAD = 6
-FIRST_SHARED = X_TILES + 2
+ORDER = [0, 1, 2, 3, 8, 4, 9, 5, 6, 7] + list(range(10, ROW_TILES))
+SPLIT_SQUARES = 2
+MATMUL_LAG = 4
+
+
+def scalar_banks(place):
+    if place < 5:
+        return 0
+    if place < 12:
+        return 1
+    return 2 if place == 12 else 3
+
 
 FLOPS = 2 * BATCH * HIDDEN * DEPTH
 
@@ -42,14 +53,14 @@ def tile_net_pa_kernel(tc, x, w1, g1, b1, out):
 
     with ExitStack() as ctx:
         const = ctx.enter_context(tc.tile_pool(name="const", bufs=1))
-        raw_pool = ctx.enter_context(tc.tile_pool(name="raw", bufs=LOADS_AHEAD + 2))
+        raw_pool = ctx.enter_context(tc.tile_pool(name="raw", bufs=LOADS_AHEAD + 4))
         squares_pool = ctx.enter_context(tc.tile_pool(name="squares", bufs=2))
         unit_pool = ctx.enter_context(tc.tile_pool(name="unit", bufs=3))
-        grouped_pool = ctx.enter_context(tc.tile_pool(name="grouped", bufs=3))
+        grouped_pool = ctx.enter_context(tc.tile_pool(name="grouped", bufs=4))
         weight_pool = ctx.enter_context(tc.tile_pool(name="weight", bufs=3))
-        small = ctx.enter_context(tc.tile_pool(name="small", bufs=4))
-        sim_pool = ctx.enter_context(tc.tile_pool(name="sim", bufs=3))
-        normed_pool = ctx.enter_context(tc.tile_pool(name="normed", bufs=2))
+        small = ctx.enter_context(tc.tile_pool(name="small", bufs=6))
+        sim_pool = ctx.enter_context(tc.tile_pool(name="sim", bufs=6))
+        normed_pool = ctx.enter_context(tc.tile_pool(name="normed", bufs=3))
         result_pool = ctx.enter_context(tc.tile_pool(name="result", bufs=6))
         turn_in_pool = ctx.enter_context(tc.psum_pool(name="turn_in", bufs=4))
         turn_out_pool = ctx.enter_context(tc.psum_pool(name="turn_out", bufs=2))
@@ -58,8 +69,6 @@ def tile_net_pa_kernel(tc, x, w1, g1, b1, out):
 
         power_half = const.tile([P, 1], F32)
         nc.vector.memset(power_half[:], 0.5)
-        power_minus_half = const.tile([P, 1], F32)
-        nc.vector.memset(power_minus_half[:], -0.5)
         power_minus_one = const.tile([P, 1], F32)
         nc.vector.memset(power_minus_one[:], -1.0)
 
@@ -70,8 +79,8 @@ def tile_net_pa_kernel(tc, x, w1, g1, b1, out):
         x_codes = const.tile([P, PASSES, BATCH], U32, align_bytes=64)
         x_scales = const.tile([P, PASSES, BATCH], U8, align_bytes=64)
 
-        raw, norm, unit, turned_in, grouped = {}, {}, {}, {}, {}
-        weights, sums, sims, counts, lines, normeds, turned_out = {}, {}, {}, {}, {}, {}, {}
+        raw, squared, norm, unit, turned_in, grouped = {}, {}, {}, {}, {}, {}
+        weights, sums, sims, counts, fits, lines, normeds, turned_out = {}, {}, {}, {}, {}, {}, {}, {}
 
         vector_rows = const.tile([P, P], BF16)
         gain_shift = const.tile([P, 2 * W_TILES], F32)
@@ -83,11 +92,16 @@ def tile_net_pa_kernel(tc, x, w1, g1, b1, out):
                 out=vector_rows[W_TILES : 2 * W_TILES, :], in_=b1.rearrange("(j n) -> j n", n=P)
             )
 
-        def spread_gain_and_shift():
-            ident_bf16 = const.tile([P, P], BF16)
-            nc.vector.tensor_copy(out=ident_bf16[:], in_=ident_f32[:])
+        ident_bf16 = const.tile([P, P], BF16)
+        turned_vectors = []
+
+        def turn_gain_and_shift():
             vector_cols = turn_out_pool.tile([P, P], BF16, tag="turned_back")
             nc.tensor.transpose(vector_cols[:], vector_rows[:], ident_bf16[:])
+            turned_vectors.append(vector_cols)
+
+        def keep_gain_and_shift():
+            vector_cols = turned_vectors[0]
             nc.vector.tensor_copy(out=gain_shift[:, 0:W_TILES], in_=vector_cols[:, 0:W_TILES])
             nc.vector.tensor_scalar_mul(
                 out=gain_shift[:, W_TILES : 2 * W_TILES],
@@ -100,14 +114,47 @@ def tile_net_pa_kernel(tc, x, w1, g1, b1, out):
             nc.sync.dma_start(out=rows[:], in_=rows_in_dram[r])
             raw[r] = rows
 
-        def measure(r):
+        def square(r):
+            width = DEPTH // 2 if r < SPLIT_SQUARES else DEPTH
             squares = squares_pool.tile([P, DEPTH], BF16)
-            sum_squares = small.tile([P, 1], F32)
+            sums_of_squares = small.tile([P, 1], F32)
             nc.scalar.activation(
-                out=squares[:], in_=raw[r][:], func=ACT.Square, accum_out=sum_squares[:]
+                out=squares[:, 0:width], in_=raw[r][:, 0:width], func=ACT.Square,
+                accum_out=sums_of_squares[:],
             )
+            squared[r] = [sums_of_squares]
+            if r < SPLIT_SQUARES:
+                other_squares = squares_pool.tile([P, DEPTH // 2], BF16)
+                other_sums = small.tile([P, 1], F32)
+                nc.vector.scalar_tensor_tensor(
+                    out=other_squares[:], in0=raw[r][:, width:], scalar=1.0, in1=raw[r][:, width:],
+                    op0=ALU.mult, op1=ALU.mult, accum_out=other_sums[:],
+                )
+                squared[r].append(other_sums)
+
+        def invert_first(r):
             length = small.tile([P, 1], F32)
-            nc.gpsimd.tensor_tensor(out=length[:], in0=sum_squares[:], in1=power_half[:], op=ALU.pow)
+            nc.scalar.activation(
+                out=length[:], in_=squared[r][0][:], func=ACT.Sqrt, bias=squared[r][1][:, 0:1]
+            )
+            padded = small.tile([P, 1], F32)
+            nc.vector.tensor_scalar(
+                out=padded[:], in0=length[:], scalar1=EPS, scalar2=1.0, op0=ALU.add, op1=ALU.mult
+            )
+            inverse = small.tile([P, 1], F32)
+            nc.vector.reciprocal(out=inverse[:], in_=padded[:])
+            norm[r] = inverse
+
+        def invert(r):
+            total = squared[r][0]
+            if r < SPLIT_SQUARES:
+                total = small.tile([P, 1], F32)
+                nc.gpsimd.tensor_scalar(
+                    out=total[:], in0=squared[r][0][:], scalar1=squared[r][1][:, 0:1], scalar2=1.0,
+                    op0=ALU.add, op1=ALU.mult,
+                )
+            length = small.tile([P, 1], F32)
+            nc.gpsimd.tensor_tensor(out=length[:], in0=total[:], in1=power_half[:], op=ALU.pow)
             padded = small.tile([P, 1], F32)
             nc.gpsimd.tensor_scalar(
                 out=padded[:], in0=length[:], scalar1=EPS, scalar2=1.0, op0=ALU.add, op1=ALU.mult
@@ -134,17 +181,20 @@ def tile_net_pa_kernel(tc, x, w1, g1, b1, out):
                     nc.tensor.transpose(turned[:, q, :], pairs[:, words], ident_f32[:])
                 turned_in[r].append(turned)
 
-        def regroup(r):
-            lined = grouped_pool.tile([P, DEPTH], BF16, align_bytes=64)
-            lined_pairs = lined[:].bitcast(F32).rearrange("p (g c u) -> p g c u", g=PASSES, u=2)
-            for m in range(BANKS):
+        def regroup(place, engine):
+            r = ORDER[place]
+            if r not in grouped:
+                lined = grouped_pool.tile([P, DEPTH], BF16, align_bytes=64)
+                grouped[r] = lined
+            lined_pairs = grouped[r][:].bitcast(F32).rearrange("p (g c u) -> p g c u", g=PASSES, u=2)
+            vector_banks = BANKS - scalar_banks(place)
+            for m in range(vector_banks) if engine == "vector" else range(vector_banks, BANKS):
                 source = turned_in[r][m][:].rearrange("p (g u) c -> p g c u", u=2)
                 target = lined_pairs[:, 2 * m : 2 * m + 2, :, :]
-                if r >= FIRST_SHARED and m > 0:
-                    nc.scalar.copy(out=target, in_=source)
-                else:
+                if engine == "vector":
                     nc.vector.tensor_copy(out=target, in_=source)
-            grouped[r] = lined
+                else:
+                    nc.scalar.copy(out=target, in_=source)
 
         def quantise(r):
             if r < X_TILES:
@@ -166,37 +216,34 @@ def tile_net_pa_kernel(tc, x, w1, g1, b1, out):
                     )
                 weights[r - X_TILES] = (w_codes, w_scales)
 
-        def multiply(j):
+        def multiply(j, h):
             w_codes, w_scales = weights[j]
-            sums[j] = []
-            for h in range(HALVES):
-                half = slice(h * N_MOVE, (h + 1) * N_MOVE)
-                acc = acc_pool.tile([P, N_MOVE], F32)
-                for g in range(PASSES):
-                    w_cols = slice(g * P, (g + 1) * P)
-                    nc.tensor.matmul_mx(
-                        out=acc[:],
-                        lhsT=w_codes[:, w_cols].bitcast(FP8X4),
-                        lhsT_scale=w_scales[:, w_cols],
-                        rhs=x_codes[:, g, half].bitcast(FP8X4),
-                        rhs_scale=x_scales[:, g, half],
-                        start=(g == 0),
-                        stop=(g == PASSES - 1),
-                    )
-                sums[j].append(acc)
+            half = slice(h * N_MOVE, (h + 1) * N_MOVE)
+            acc = acc_pool.tile([P, N_MOVE], F32)
+            for g in range(PASSES):
+                w_cols = slice(g * P, (g + 1) * P)
+                nc.tensor.matmul_mx(
+                    out=acc[:],
+                    lhsT=w_codes[:, w_cols].bitcast(FP8X4),
+                    lhsT_scale=w_scales[:, w_cols],
+                    rhs=x_codes[:, g, half].bitcast(FP8X4),
+                    rhs_scale=x_scales[:, g, half],
+                    start=(g == 0),
+                    stop=(g == PASSES - 1),
+                )
+            sums[j, h] = acc
 
         def clip(j, h):
-            if h == 0:
+            if j not in sims:
                 sim = sim_pool.tile([P, BATCH], F32)
                 sims[j] = sim
-            half_cols = slice(h * N_MOVE, (h + 1) * N_MOVE)
             nc.vector.tensor_scalar(
-                out=sims[j][:, half_cols], in0=sums[j][h][:], scalar1=0.0, scalar2=1.0,
-                op0=ALU.max, op1=ALU.min,
+                out=sims[j][:, h * N_MOVE : (h + 1) * N_MOVE], in0=sums[j, h][:],
+                scalar1=0.0, scalar2=1.0, op0=ALU.max, op1=ALU.min,
             )
 
         def count(j, h):
-            if h == 0:
+            if j not in counts:
                 stats = small.tile([P, HALVES, 6], F32)
                 counts[j] = stats
             nc.vector.bn_stats(
@@ -206,26 +253,33 @@ def tile_net_pa_kernel(tc, x, w1, g1, b1, out):
         def fit(j):
             mean_var = small.tile([P, 2], F32)
             nc.vector.bn_aggr(out=mean_var[:], in_=counts[j][:].rearrange("p h s -> p (h s)"))
-            padded_var = small.tile([P, 1], F32)
-            nc.gpsimd.tensor_scalar(
-                out=padded_var[:], in0=mean_var[:, 1:2], scalar1=BN_EPS, scalar2=1.0,
-                op0=ALU.add, op1=ALU.mult,
-            )
+            fits[j] = mean_var
+
+        def take_root(j):
+            std = small.tile([P, 1], F32)
+            nc.scalar.activation(out=std[:], in_=fits[j][:, 1:2], func=ACT.Sqrt, bias=BN_EPS)
+            lines[j] = [std]
+
+        def invert_std(j):
             inverse_std = small.tile([P, 1], F32)
-            nc.gpsimd.tensor_tensor(
-                out=inverse_std[:], in0=padded_var[:], in1=power_minus_half[:], op=ALU.pow
-            )
+            nc.vector.reciprocal(out=inverse_std[:], in_=lines[j][0][:])
+            lines[j] = [inverse_std]
+
+        def make_slope(j):
             slope = small.tile([P, 1], F32)
-            nc.gpsimd.tensor_tensor(
-                out=slope[:], in0=inverse_std[:], in1=gain_shift[:, j : j + 1], op=ALU.mult
+            nc.vector.tensor_scalar_mul(
+                out=slope[:], in0=lines[j][0][:], scalar1=gain_shift[:, j : j + 1]
             )
+            lines[j] = [slope]
+
+        def make_drop(j):
             drop = small.tile([P, 1], F32)
-            nc.gpsimd.tensor_scalar(
-                out=drop[:], in0=mean_var[:, 0:1], scalar1=slope[:, 0:1],
+            nc.vector.tensor_scalar(
+                out=drop[:], in0=fits[j][:, 0:1], scalar1=lines[j][0][:, 0:1],
                 scalar2=gain_shift[:, W_TILES + j : W_TILES + j + 1],
                 op0=ALU.mult, op1=ALU.add,
             )
-            lines[j] = (slope, drop)
+            lines[j].append(drop)
 
         def normalise(j):
             slope, drop = lines[j]
@@ -258,41 +312,73 @@ def tile_net_pa_kernel(tc, x, w1, g1, b1, out):
                     out=out_tiles[j][:, PER_BANK * m : PER_BANK * (m + 1), :], in_=result[:]
                 )
 
-        for r in range(LOADS_AHEAD):
-            load(r)
+        place_of = {ORDER[place]: place for place in range(ROW_TILES)}
+        matmuls = {}
+        for j in range(W_TILES):
+            for h in range(HALVES):
+                images = range(h * PER_BANK, (h + 1) * PER_BANK)
+                last = max([place_of[X_TILES + j]] + [place_of[i] for i in images])
+                matmuls.setdefault(last + MATMUL_LAG, []).append((j, h))
+        fitted_in = {}
+        for step in matmuls:
+            for n, (j, h) in enumerate(matmuls[step]):
+                fitted_in[j] = max(fitted_in.get(j, 0), step + 1 + n)
+
+        def tiles_at(step, lag):
+            return [j for j in range(W_TILES) if fitted_in[j] + lag == step]
+
+        for place in range(LOADS_AHEAD):
+            load(ORDER[place])
         load_gain_and_shift()
-        for step in range(ROW_TILES + 6):
-            scaled_now = step - 1
-            grouped_now = step - 2
-            multiplied_now = step - 3 - X_TILES
-            fitted_now = step - 4 - X_TILES
-            stored_now = step - 5 - X_TILES
-            if 0 <= multiplied_now < W_TILES:
-                multiply(multiplied_now)
-            if 0 <= fitted_now < W_TILES:
-                count(fitted_now, 1)
-            if 0 <= grouped_now < ROW_TILES:
-                regroup(grouped_now)
-            if 0 <= fitted_now < W_TILES:
-                fit(fitted_now)
-            if step < ROW_TILES:
-                measure(step)
-            if 0 <= stored_now < W_TILES:
-                normalise(stored_now)
-                turn_back(stored_now)
-            if 0 <= scaled_now < ROW_TILES:
-                scale(scaled_now)
-                turn(scaled_now)
-            if 0 <= multiplied_now < W_TILES:
-                clip(multiplied_now, 0)
-            if 0 <= grouped_now < ROW_TILES:
-                quantise(grouped_now)
-            if 0 <= multiplied_now < W_TILES:
-                clip(multiplied_now, 1)
-                count(multiplied_now, 0)
-            if 0 <= stored_now < W_TILES:
-                store(stored_now)
+        square(ORDER[0])
+        invert_first(ORDER[0])
+        for step in range(max(fitted_in.values()) + 4):
+            now = matmuls.get(step, [])
+            before = matmuls.get(step - 1, [])
+            for j in tiles_at(step, 0):
+                fit(j)
+            if 0 <= step - 3 < ROW_TILES:
+                regroup(step - 3, "vector")
+            for j, h in before[1:]:
+                clip(j, h)
+            for j in tiles_at(step, 3):
+                turn_back(j)
+            for j, h in now:
+                multiply(j, h)
+            if 0 <= step - 2 < ROW_TILES:
+                turn(ORDER[step - 2])
+            for j in tiles_at(step, 3):
+                store(j)
+            if 0 <= step - 2 < ROW_TILES:
+                regroup(step - 2, "scalar")
+            for j in tiles_at(step, 0):
+                take_root(j)
+            if step + 1 < ROW_TILES:
+                square(ORDER[step + 1])
+                invert(ORDER[step + 1])
+            if 0 <= step - 3 < ROW_TILES:
+                quantise(ORDER[step - 3])
+            for j in tiles_at(step, 1):
+                invert_std(j)
+            for j in tiles_at(step, 2):
+                normalise(j)
+            for j in tiles_at(step, 1):
+                make_slope(j)
+            for j, h in before[1:]:
+                count(j, h)
+            for j, h in now[:1]:
+                clip(j, h)
+            for j in tiles_at(step, 1):
+                make_drop(j)
+            if 0 <= step - 1 < ROW_TILES:
+                scale(ORDER[step - 1])
+            for j, h in now[:1]:
+                count(j, h)
             if step + LOADS_AHEAD < ROW_TILES:
-                load(step + LOADS_AHEAD)
-            if step == X_TILES:
-                spread_gain_and_shift()
+                load(ORDER[step + LOADS_AHEAD])
+            if step == 2:
+                nc.gpsimd.tensor_copy(out=ident_bf16[:], in_=ident_f32[:])
+            if step == 3:
+                turn_gain_and_shift()
+            if step == 4:
+                keep_gain_and_shift()

@@ -29,16 +29,14 @@ EPS = 1e-12
 BN_EPS = 1e-5
 LOADS_AHEAD = 6
 ORDER = [0, 1, 2, 3, 8, 4, 9, 5, 6, 7] + list(range(10, ROW_TILES))
+FIRST_REORDERED = 12
 SPLIT_SQUARES = 2
-MATMUL_LAG = 4
+MATMUL_LAG = 3
+LINE_LAG = 3
 
 
 def scalar_banks(place):
-    if place < 5:
-        return 0
-    if place < 12:
-        return 1
-    return 2 if place == 12 else 3
+    return 0 if place < 4 else 1 if place < 9 else 2 if place < 13 else 3
 
 
 FLOPS = 2 * BATCH * HIDDEN * DEPTH
@@ -67,8 +65,15 @@ def tile_net_pa_kernel(tc, x, w1, g1, b1, out):
         acc_pool = ctx.enter_context(tc.psum_pool(name="acc", bufs=2))
         ctx.enter_context(tc.manual_schedule())
 
+        one = const.tile([P, 1], F32)
+        nc.vector.memset(one[:], 1.0)
+        table_loaded = const.tile([P, 1], F32)
+        nc.scalar.activation(out=table_loaded[:], in_=one[:], func=ACT.Sqrt)
+
         power_half = const.tile([P, 1], F32)
         nc.vector.memset(power_half[:], 0.5)
+        power_minus_half = const.tile([P, 1], F32)
+        nc.vector.memset(power_minus_half[:], -0.5)
         power_minus_one = const.tile([P, 1], F32)
         nc.vector.memset(power_minus_one[:], -1.0)
 
@@ -132,29 +137,30 @@ def tile_net_pa_kernel(tc, x, w1, g1, b1, out):
                 )
                 squared[r].append(other_sums)
 
-        def invert_first(r):
-            length = small.tile([P, 1], F32)
-            nc.scalar.activation(
-                out=length[:], in_=squared[r][0][:], func=ACT.Sqrt, bias=squared[r][1][:, 0:1]
-            )
-            padded = small.tile([P, 1], F32)
-            nc.vector.tensor_scalar(
-                out=padded[:], in0=length[:], scalar1=EPS, scalar2=1.0, op0=ALU.add, op1=ALU.mult
-            )
-            inverse = small.tile([P, 1], F32)
-            nc.vector.reciprocal(out=inverse[:], in_=padded[:])
-            norm[r] = inverse
+        def invert_first():
+            lengths, padded, inverses = [], [], []
+            for r in range(SPLIT_SQUARES):
+                length = const.tile([P, 1], F32, name="length" + str(r))
+                nc.scalar.activation(
+                    out=length[:], in_=squared[r][0][:], func=ACT.Sqrt, bias=squared[r][1][:, 0:1]
+                )
+                lengths.append(length)
+            for r in range(SPLIT_SQUARES):
+                plus = const.tile([P, 1], F32, name="plus" + str(r))
+                nc.vector.tensor_scalar(
+                    out=plus[:], in0=lengths[r][:], scalar1=EPS, scalar2=1.0, op0=ALU.add, op1=ALU.mult
+                )
+                padded.append(plus)
+            for r in range(SPLIT_SQUARES):
+                inverse = const.tile([P, 1], F32, name="inverse" + str(r))
+                nc.vector.reciprocal(out=inverse[:], in_=padded[r][:])
+                norm[r] = inverse
 
         def invert(r):
-            total = squared[r][0]
-            if r < SPLIT_SQUARES:
-                total = small.tile([P, 1], F32)
-                nc.gpsimd.tensor_scalar(
-                    out=total[:], in0=squared[r][0][:], scalar1=squared[r][1][:, 0:1], scalar2=1.0,
-                    op0=ALU.add, op1=ALU.mult,
-                )
             length = small.tile([P, 1], F32)
-            nc.gpsimd.tensor_tensor(out=length[:], in0=total[:], in1=power_half[:], op=ALU.pow)
+            nc.gpsimd.tensor_tensor(
+                out=length[:], in0=squared[r][0][:], in1=power_half[:], op=ALU.pow
+            )
             padded = small.tile([P, 1], F32)
             nc.gpsimd.tensor_scalar(
                 out=padded[:], in0=length[:], scalar1=EPS, scalar2=1.0, op0=ALU.add, op1=ALU.mult
@@ -165,19 +171,31 @@ def tile_net_pa_kernel(tc, x, w1, g1, b1, out):
             )
             norm[r] = inverse
 
-        def scale(r):
+        def scale(place):
+            r = ORDER[place]
             scaled = unit_pool.tile([P, DEPTH], BF16)
-            nc.vector.tensor_scalar_mul(out=scaled[:], in0=raw[r][:], scalar1=norm[r][:, 0:1])
+            if place < FIRST_REORDERED:
+                nc.vector.tensor_scalar_mul(out=scaled[:], in0=raw[r][:], scalar1=norm[r][:, 0:1])
+            else:
+                nc.vector.tensor_scalar_mul(
+                    out=scaled[:].rearrange("p (u w e) -> p u w e", u=2, e=2),
+                    in0=raw[r][:].rearrange("p (w u e) -> p u w e", u=2, e=2),
+                    scalar1=norm[r][:, 0:1],
+                )
             unit[r] = scaled
 
-        def turn(r):
+        def turn(place):
+            r = ORDER[place]
             pairs = unit[r][:].bitcast(F32)
             turned_in[r] = []
             for m in range(BANKS):
                 turned = turn_in_pool.tile([P, PER_BANK, P], F32)
                 for q in range(PER_BANK):
                     g, u = divmod(PER_BANK * m + q, 2)
-                    words = slice(2 * P * g + u, 2 * P * (g + 1), 2)
+                    if place < FIRST_REORDERED:
+                        words = slice(2 * P * g + u, 2 * P * (g + 1), 2)
+                    else:
+                        words = slice((u * PASSES + g) * P, (u * PASSES + g + 1) * P)
                     nc.tensor.transpose(turned[:, q, :], pairs[:, words], ident_f32[:])
                 turned_in[r].append(turned)
 
@@ -216,38 +234,40 @@ def tile_net_pa_kernel(tc, x, w1, g1, b1, out):
                     )
                 weights[r - X_TILES] = (w_codes, w_scales)
 
-        def multiply(j, h):
+        def multiply(j, first, width):
             w_codes, w_scales = weights[j]
-            half = slice(h * N_MOVE, (h + 1) * N_MOVE)
+            images = slice(first, first + width)
             acc = acc_pool.tile([P, N_MOVE], F32)
             for g in range(PASSES):
                 w_cols = slice(g * P, (g + 1) * P)
                 nc.tensor.matmul_mx(
-                    out=acc[:],
+                    out=acc[:, 0:width],
                     lhsT=w_codes[:, w_cols].bitcast(FP8X4),
                     lhsT_scale=w_scales[:, w_cols],
-                    rhs=x_codes[:, g, half].bitcast(FP8X4),
-                    rhs_scale=x_scales[:, g, half],
+                    rhs=x_codes[:, g, images].bitcast(FP8X4),
+                    rhs_scale=x_scales[:, g, images],
                     start=(g == 0),
                     stop=(g == PASSES - 1),
                 )
-            sums[j, h] = acc
+            sums[j, first] = acc
 
-        def clip(j, h):
+        def clip(j, first, width):
             if j not in sims:
                 sim = sim_pool.tile([P, BATCH], F32)
                 sims[j] = sim
             nc.vector.tensor_scalar(
-                out=sims[j][:, h * N_MOVE : (h + 1) * N_MOVE], in0=sums[j, h][:],
+                out=sims[j][:, first : first + width], in0=sums[j, first][:, 0:width],
                 scalar1=0.0, scalar2=1.0, op0=ALU.max, op1=ALU.min,
             )
 
-        def count(j, h):
+        def count(j, first, width):
+            parts = [part for part in chunks[j]]
             if j not in counts:
-                stats = small.tile([P, HALVES, 6], F32)
+                stats = small.tile([P, len(parts), 6], F32, name="stats" + str(len(parts)))
                 counts[j] = stats
             nc.vector.bn_stats(
-                out=counts[j][:, h, :], in_=sims[j][:, h * N_MOVE : (h + 1) * N_MOVE]
+                out=counts[j][:, parts.index((first, width)), :],
+                in_=sims[j][:, first : first + width],
             )
 
         def fit(j):
@@ -255,31 +275,27 @@ def tile_net_pa_kernel(tc, x, w1, g1, b1, out):
             nc.vector.bn_aggr(out=mean_var[:], in_=counts[j][:].rearrange("p h s -> p (h s)"))
             fits[j] = mean_var
 
-        def take_root(j):
-            std = small.tile([P, 1], F32)
-            nc.scalar.activation(out=std[:], in_=fits[j][:, 1:2], func=ACT.Sqrt, bias=BN_EPS)
-            lines[j] = [std]
-
-        def invert_std(j):
-            inverse_std = small.tile([P, 1], F32)
-            nc.vector.reciprocal(out=inverse_std[:], in_=lines[j][0][:])
-            lines[j] = [inverse_std]
-
-        def make_slope(j):
-            slope = small.tile([P, 1], F32)
-            nc.vector.tensor_scalar_mul(
-                out=slope[:], in0=lines[j][0][:], scalar1=gain_shift[:, j : j + 1]
+        def make_line(j):
+            padded_var = small.tile([P, 1], F32)
+            nc.gpsimd.tensor_scalar(
+                out=padded_var[:], in0=fits[j][:, 1:2], scalar1=BN_EPS, scalar2=1.0,
+                op0=ALU.add, op1=ALU.mult,
             )
-            lines[j] = [slope]
-
-        def make_drop(j):
+            inverse_std = small.tile([P, 1], F32)
+            nc.gpsimd.tensor_tensor(
+                out=inverse_std[:], in0=padded_var[:], in1=power_minus_half[:], op=ALU.pow
+            )
+            slope = small.tile([P, 1], F32)
+            nc.gpsimd.tensor_tensor(
+                out=slope[:], in0=inverse_std[:], in1=gain_shift[:, j : j + 1], op=ALU.mult
+            )
             drop = small.tile([P, 1], F32)
-            nc.vector.tensor_scalar(
-                out=drop[:], in0=fits[j][:, 0:1], scalar1=lines[j][0][:, 0:1],
+            nc.gpsimd.tensor_scalar(
+                out=drop[:], in0=fits[j][:, 0:1], scalar1=slope[:, 0:1],
                 scalar2=gain_shift[:, W_TILES + j : W_TILES + j + 1],
                 op0=ALU.mult, op1=ALU.add,
             )
-            lines[j].append(drop)
+            lines[j] = (slope, drop)
 
         def normalise(j):
             slope, drop = lines[j]
@@ -313,16 +329,20 @@ def tile_net_pa_kernel(tc, x, w1, g1, b1, out):
                 )
 
         place_of = {ORDER[place]: place for place in range(ROW_TILES)}
-        matmuls = {}
+        chunks, matmuls, fitted_in = {}, {}, {}
         for j in range(W_TILES):
-            for h in range(HALVES):
-                images = range(h * PER_BANK, (h + 1) * PER_BANK)
-                last = max([place_of[X_TILES + j]] + [place_of[i] for i in images])
-                matmuls.setdefault(last + MATMUL_LAG, []).append((j, h))
-        fitted_in = {}
+            early = place_of[X_TILES + j] < place_of[X_TILES - 1]
+            quarter = N_MOVE // 2
+            chunks[j] = [(0, N_MOVE)]
+            chunks[j] += [(N_MOVE, quarter), (N_MOVE + quarter, quarter)] if early else [(N_MOVE, N_MOVE)]
+        for j in range(W_TILES):
+            for first, width in chunks[j]:
+                needed = [place_of[i] for i in range(first // P, (first + width) // P)]
+                step = max(needed + [place_of[X_TILES + j]]) + MATMUL_LAG
+                matmuls.setdefault(step, []).append((j, first, width))
         for step in matmuls:
-            for n, (j, h) in enumerate(matmuls[step]):
-                fitted_in[j] = max(fitted_in.get(j, 0), step + 1 + n)
+            for n, part in enumerate(matmuls[step]):
+                fitted_in[part[0]] = max(fitted_in.get(part[0], 0), step + 1 + n)
 
         def tiles_at(step, lag):
             return [j for j in range(W_TILES) if fitted_in[j] + lag == step]
@@ -330,52 +350,46 @@ def tile_net_pa_kernel(tc, x, w1, g1, b1, out):
         for place in range(LOADS_AHEAD):
             load(ORDER[place])
         load_gain_and_shift()
-        square(ORDER[0])
-        invert_first(ORDER[0])
-        for step in range(max(fitted_in.values()) + 4):
+        for r in range(SPLIT_SQUARES):
+            square(r)
+        invert_first()
+        for step in range(1, max(fitted_in.values()) + LINE_LAG + 1):
             now = matmuls.get(step, [])
             before = matmuls.get(step - 1, [])
+            for part in before[1:]:
+                clip(*part)
+            if step - 1 < ROW_TILES:
+                scale(step - 1)
+            if 0 <= step - 2 < ROW_TILES:
+                regroup(step - 2, "vector")
             for j in tiles_at(step, 0):
                 fit(j)
-            if 0 <= step - 3 < ROW_TILES:
-                regroup(step - 3, "vector")
-            for j, h in before[1:]:
-                clip(j, h)
-            for j in tiles_at(step, 3):
+                make_line(j)
+            for j in tiles_at(step, LINE_LAG):
+                normalise(j)
+            for part in now:
+                multiply(*part)
+            for j in tiles_at(step, LINE_LAG):
                 turn_back(j)
-            for j, h in now:
-                multiply(j, h)
-            if 0 <= step - 2 < ROW_TILES:
-                turn(ORDER[step - 2])
-            for j in tiles_at(step, 3):
-                store(j)
-            if 0 <= step - 2 < ROW_TILES:
-                regroup(step - 2, "scalar")
-            for j in tiles_at(step, 0):
-                take_root(j)
+            if step - 1 < ROW_TILES:
+                turn(step - 1)
             if step + 1 < ROW_TILES:
                 square(ORDER[step + 1])
                 invert(ORDER[step + 1])
-            if 0 <= step - 3 < ROW_TILES:
-                quantise(ORDER[step - 3])
-            for j in tiles_at(step, 1):
-                invert_std(j)
-            for j in tiles_at(step, 2):
-                normalise(j)
-            for j in tiles_at(step, 1):
-                make_slope(j)
-            for j, h in before[1:]:
-                count(j, h)
-            for j, h in now[:1]:
-                clip(j, h)
-            for j in tiles_at(step, 1):
-                make_drop(j)
-            if 0 <= step - 1 < ROW_TILES:
-                scale(ORDER[step - 1])
-            for j, h in now[:1]:
-                count(j, h)
-            if step + LOADS_AHEAD < ROW_TILES:
-                load(ORDER[step + LOADS_AHEAD])
+            if step - 1 < ROW_TILES:
+                regroup(step - 1, "scalar")
+            for j in tiles_at(step, LINE_LAG):
+                store(j)
+            for part in now[:1]:
+                clip(*part)
+            for part in before[1:]:
+                count(*part)
+            if 0 <= step - 2 < ROW_TILES:
+                quantise(ORDER[step - 2])
+            for part in now[:1]:
+                count(*part)
+            if step - 1 + LOADS_AHEAD < ROW_TILES:
+                load(ORDER[step - 1 + LOADS_AHEAD])
             if step == 2:
                 nc.gpsimd.tensor_copy(out=ident_bf16[:], in_=ident_f32[:])
             if step == 3:

@@ -32,7 +32,7 @@ ORDER = [0, 1, 2, 3, 8, 4, 9, 5, 6, 7] + list(range(10, ROW_TILES))
 FIRST_REORDERED = 12
 SPLIT_SQUARES = 2
 MATMUL_LAG = 3
-LINE_LAG = 3
+LINE_LAG = 2
 
 
 def scalar_banks(place):
@@ -69,13 +69,6 @@ def tile_net_pa_kernel(tc, x, w1, g1, b1, out):
         nc.vector.memset(one[:], 1.0)
         table_loaded = const.tile([P, 1], F32)
         nc.scalar.activation(out=table_loaded[:], in_=one[:], func=ACT.Sqrt)
-
-        power_half = const.tile([P, 1], F32)
-        nc.vector.memset(power_half[:], 0.5)
-        power_minus_half = const.tile([P, 1], F32)
-        nc.vector.memset(power_minus_half[:], -0.5)
-        power_minus_one = const.tile([P, 1], F32)
-        nc.vector.memset(power_minus_one[:], -1.0)
 
         ident_f32 = const.tile([P, P], F32)
         nc.vector.memset(ident_f32[:], 0.0)
@@ -156,19 +149,21 @@ def tile_net_pa_kernel(tc, x, w1, g1, b1, out):
                 nc.vector.reciprocal(out=inverse[:], in_=padded[r][:])
                 norm[r] = inverse
 
-        def invert(r):
+        def take_length(r):
             length = small.tile([P, 1], F32)
-            nc.gpsimd.tensor_tensor(
-                out=length[:], in0=squared[r][0][:], in1=power_half[:], op=ALU.pow
-            )
+            nc.scalar.activation(out=length[:], in_=squared[r][0][:], func=ACT.Sqrt)
+            norm[r] = length
+
+        def pad_length(r):
             padded = small.tile([P, 1], F32)
-            nc.gpsimd.tensor_scalar(
-                out=padded[:], in0=length[:], scalar1=EPS, scalar2=1.0, op0=ALU.add, op1=ALU.mult
+            nc.vector.tensor_scalar(
+                out=padded[:], in0=norm[r][:], scalar1=EPS, scalar2=1.0, op0=ALU.add, op1=ALU.mult
             )
+            norm[r] = padded
+
+        def invert_length(r):
             inverse = small.tile([P, 1], F32)
-            nc.gpsimd.tensor_tensor(
-                out=inverse[:], in0=padded[:], in1=power_minus_one[:], op=ALU.pow
-            )
+            nc.vector.reciprocal(out=inverse[:], in_=norm[r][:])
             norm[r] = inverse
 
         def scale(place):
@@ -275,27 +270,31 @@ def tile_net_pa_kernel(tc, x, w1, g1, b1, out):
             nc.vector.bn_aggr(out=mean_var[:], in_=counts[j][:].rearrange("p h s -> p (h s)"))
             fits[j] = mean_var
 
-        def make_line(j):
-            padded_var = small.tile([P, 1], F32)
-            nc.gpsimd.tensor_scalar(
-                out=padded_var[:], in0=fits[j][:, 1:2], scalar1=BN_EPS, scalar2=1.0,
-                op0=ALU.add, op1=ALU.mult,
-            )
+        def take_std(j):
+            std = small.tile([P, 1], F32)
+            nc.scalar.activation(out=std[:], in_=fits[j][:, 1:2], func=ACT.Sqrt, bias=BN_EPS)
+            lines[j] = [std]
+
+        def invert_std(j):
             inverse_std = small.tile([P, 1], F32)
-            nc.gpsimd.tensor_tensor(
-                out=inverse_std[:], in0=padded_var[:], in1=power_minus_half[:], op=ALU.pow
-            )
+            nc.vector.reciprocal(out=inverse_std[:], in_=lines[j][0][:])
+            lines[j] = [inverse_std]
+
+        def make_slope(j):
             slope = small.tile([P, 1], F32)
-            nc.gpsimd.tensor_tensor(
-                out=slope[:], in0=inverse_std[:], in1=gain_shift[:, j : j + 1], op=ALU.mult
+            nc.vector.tensor_scalar_mul(
+                out=slope[:], in0=lines[j][0][:], scalar1=gain_shift[:, j : j + 1]
             )
+            lines[j] = [slope]
+
+        def make_drop(j):
             drop = small.tile([P, 1], F32)
-            nc.gpsimd.tensor_scalar(
-                out=drop[:], in0=fits[j][:, 0:1], scalar1=slope[:, 0:1],
+            nc.vector.tensor_scalar(
+                out=drop[:], in0=fits[j][:, 0:1], scalar1=lines[j][0][:, 0:1],
                 scalar2=gain_shift[:, W_TILES + j : W_TILES + j + 1],
                 op0=ALU.mult, op1=ALU.add,
             )
-            lines[j] = (slope, drop)
+            lines[j].append(drop)
 
         def normalise(j):
             slope, drop = lines[j]
@@ -360,13 +359,18 @@ def tile_net_pa_kernel(tc, x, w1, g1, b1, out):
                 clip(*part)
             if step - 1 < ROW_TILES:
                 scale(step - 1)
+            for j in tiles_at(step, 1):
+                invert_std(j)
             if 0 <= step - 2 < ROW_TILES:
                 regroup(step - 2, "vector")
             for j in tiles_at(step, 0):
                 fit(j)
-                make_line(j)
+            if SPLIT_SQUARES <= step < ROW_TILES:
+                pad_length(ORDER[step])
             for j in tiles_at(step, LINE_LAG):
                 normalise(j)
+            for j in tiles_at(step, 1):
+                make_slope(j)
             for part in now:
                 multiply(*part)
             for j in tiles_at(step, LINE_LAG):
@@ -375,9 +379,12 @@ def tile_net_pa_kernel(tc, x, w1, g1, b1, out):
                 turn(step - 1)
             if step + 1 < ROW_TILES:
                 square(ORDER[step + 1])
-                invert(ORDER[step + 1])
             if step - 1 < ROW_TILES:
                 regroup(step - 1, "scalar")
+            if step + 1 < ROW_TILES:
+                take_length(ORDER[step + 1])
+            for j in tiles_at(step, 0):
+                take_std(j)
             for j in tiles_at(step, LINE_LAG):
                 store(j)
             for part in now[:1]:
@@ -386,6 +393,10 @@ def tile_net_pa_kernel(tc, x, w1, g1, b1, out):
                 count(*part)
             if 0 <= step - 2 < ROW_TILES:
                 quantise(ORDER[step - 2])
+            if SPLIT_SQUARES <= step < ROW_TILES:
+                invert_length(ORDER[step])
+            for j in tiles_at(step, 1):
+                make_drop(j)
             for part in now[:1]:
                 count(*part)
             if step - 1 + LOADS_AHEAD < ROW_TILES:

@@ -29,7 +29,7 @@ EPS = 1e-12
 BN_EPS = 1e-5
 LOADS_AHEAD = 6
 ORDER = [0, 1, 2, 3, 8, 4, 9, 5, 6, 7] + list(range(10, ROW_TILES))
-FIRST_REORDERED = 12
+FIRST_REORDERED = 8
 SPLIT_SQUARES = 2
 MATMUL_LAG = 3
 LINE_LAG = 2
@@ -74,8 +74,8 @@ def tile_net_pa_kernel(tc, x, w1, g1, b1, out):
         nc.vector.memset(ident_f32[:], 0.0)
         masks.make_identity(nc, ident_f32[:], nomemset=True)
 
-        x_codes = const.tile([P, PASSES, BATCH], U32, align_bytes=64)
-        x_scales = const.tile([P, PASSES, BATCH], U8, align_bytes=64)
+        x_codes = const.tile([P, PASSES, BATCH], U32, align_bytes=256)
+        x_scales = const.tile([P, PASSES, BATCH], U8, align_bytes=256)
 
         raw, squared, norm, unit, turned_in, grouped = {}, {}, {}, {}, {}, {}
         weights, sums, sims, counts, fits, lines, normeds, turned_out = {}, {}, {}, {}, {}, {}, {}, {}
@@ -109,7 +109,10 @@ def tile_net_pa_kernel(tc, x, w1, g1, b1, out):
 
         def load(r):
             rows = raw_pool.tile([P, DEPTH], BF16)
-            nc.sync.dma_start(out=rows[:], in_=rows_in_dram[r])
+            width = DEPTH // 2 if r < SPLIT_SQUARES else DEPTH
+            for first in range(0, DEPTH, width):
+                cols = slice(first, first + width)
+                nc.sync.dma_start(out=rows[:, cols], in_=rows_in_dram[r][:, cols])
             raw[r] = rows
 
         def square(r):
@@ -197,7 +200,7 @@ def tile_net_pa_kernel(tc, x, w1, g1, b1, out):
         def regroup(place, engine):
             r = ORDER[place]
             if r not in grouped:
-                lined = grouped_pool.tile([P, DEPTH], BF16, align_bytes=64)
+                lined = grouped_pool.tile([P, DEPTH], BF16, align_bytes=256)
                 grouped[r] = lined
             lined_pairs = grouped[r][:].bitcast(F32).rearrange("p (g c u) -> p g c u", g=PASSES, u=2)
             vector_banks = BANKS - scalar_banks(place)
@@ -219,8 +222,8 @@ def tile_net_pa_kernel(tc, x, w1, g1, b1, out):
                         in_=grouped[r][:, g * K_PASS : (g + 1) * K_PASS],
                     )
             else:
-                w_codes = weight_pool.tile([P, PASSES * P], U32, align_bytes=64)
-                w_scales = weight_pool.tile([P, PASSES * P], U8, align_bytes=64)
+                w_codes = weight_pool.tile([P, PASSES * P], U32, align_bytes=256)
+                w_scales = weight_pool.tile([P, PASSES * P], U8, align_bytes=256)
                 for first, width in ((0, 4 * P), (4 * P, 2 * P)):
                     nc.vector.quantize_mx(
                         out=w_codes[:, first : first + width].bitcast(FP8X4),

@@ -32,6 +32,7 @@ ORDER = [0, 1, 2, 3, 8, 4, 9, 5, 6, 7] + list(range(10, ROW_TILES))
 FIRST_REORDERED = 8
 SPLIT_SQUARES = 2
 MATMUL_LAG = 3
+FIRST_SPREAD = 2
 LINE_LAG = 2
 
 
@@ -58,8 +59,8 @@ def tile_net_pa_kernel(tc, x, w1, g1, b1, out):
         weight_pool = ctx.enter_context(tc.tile_pool(name="weight", bufs=3))
         small = ctx.enter_context(tc.tile_pool(name="small", bufs=6))
         sim_pool = ctx.enter_context(tc.tile_pool(name="sim", bufs=6))
-        normed_pool = ctx.enter_context(tc.tile_pool(name="normed", bufs=3))
-        result_pool = ctx.enter_context(tc.tile_pool(name="result", bufs=6))
+        normed_pool = ctx.enter_context(tc.tile_pool(name="normed", bufs=4))
+        result_pool = ctx.enter_context(tc.tile_pool(name="result", bufs=8))
         turn_in_pool = ctx.enter_context(tc.psum_pool(name="turn_in", bufs=4))
         turn_out_pool = ctx.enter_context(tc.psum_pool(name="turn_out", bufs=2))
         acc_pool = ctx.enter_context(tc.psum_pool(name="acc", bufs=2))
@@ -187,7 +188,7 @@ def tile_net_pa_kernel(tc, x, w1, g1, b1, out):
             pairs = unit[r][:].bitcast(F32)
             turned_in[r] = []
             for m in range(BANKS):
-                turned = turn_in_pool.tile([P, PER_BANK, P], F32)
+                turned = turn_in_pool.tile([P, PER_BANK, P], F32, tag="turned")
                 for q in range(PER_BANK):
                     g, u = divmod(PER_BANK * m + q, 2)
                     if place < FIRST_REORDERED:
@@ -314,7 +315,10 @@ def tile_net_pa_kernel(tc, x, w1, g1, b1, out):
         def turn_back(j):
             turned_out[j] = []
             for m in range(X_TILES // PER_BANK):
-                turned_back = turn_out_pool.tile([P, PER_BANK, P], F32)
+                if m > 0 and j >= FIRST_SPREAD:
+                    turned_back = turn_in_pool.tile([P, PER_BANK, P], F32, tag="turned")
+                else:
+                    turned_back = turn_out_pool.tile([P, PER_BANK, P], F32, tag="turned_back")
                 for q in range(PER_BANK):
                     t = PER_BANK * m + q
                     nc.tensor.transpose(
@@ -325,7 +329,10 @@ def tile_net_pa_kernel(tc, x, w1, g1, b1, out):
         def store(j):
             for m in range(X_TILES // PER_BANK):
                 result = result_pool.tile([P, PER_BANK, P], F32)
-                nc.scalar.copy(out=result[:], in_=turned_out[j][m][:])
+                if m == 1 and j == W_TILES - 1:
+                    nc.vector.tensor_copy(out=result[:], in_=turned_out[j][m][:])
+                else:
+                    nc.scalar.copy(out=result[:], in_=turned_out[j][m][:])
                 nc.sync.dma_start(
                     out=out_tiles[j][:, PER_BANK * m : PER_BANK * (m + 1), :], in_=result[:]
                 )

@@ -37,7 +37,7 @@ LINE_LAG = 2
 
 
 def scalar_banks(place):
-    return 0 if place < 4 else 1 if place < 9 else 2 if place < 13 else 3
+    return 0 if place < 5 else 1 if place < 12 else 3
 
 
 FLOPS = 2 * BATCH * HIDDEN * DEPTH

from contextlib import ExitStack

import concourse.masks as masks
import concourse.mybir as mybir

F32 = mybir.dt.float32
BF16 = mybir.dt.bfloat16
U32 = mybir.dt.uint32
U8 = mybir.dt.uint8
FP8X4 = mybir.dt.float8_e4m3fn_x4
ALU = mybir.AluOpType
ACT = mybir.ActivationFunctionType

P = 128
PACK = 4
K_PASS = P * PACK
BATCH = 1024
HIDDEN = 1024
DEPTH = 3072
PASSES = DEPTH // K_PASS
X_TILES = BATCH // P
W_TILES = HIDDEN // P
ROW_TILES = X_TILES + W_TILES
PER_BANK = 4
BANKS = DEPTH // 2 // (P * PER_BANK)
N_MOVE = 512
HALVES = BATCH // N_MOVE
EPS = 1e-12
BN_EPS = 1e-5
LOADS_AHEAD = 6
ORDER = [0, 1, 2, 3, 8, 4, 9, 5, 6, 7] + list(range(10, ROW_TILES))
FIRST_REORDERED = 8
SPLIT_SQUARES = 2
MATMUL_LAG = 3
FIRST_SPREAD = 2
LINE_LAG = 2


def scalar_banks(place):
    return 0 if place < 5 else 1 if place < 12 else 3


FLOPS = 2 * BATCH * HIDDEN * DEPTH


def tile_net_pa_kernel(tc, x, w1, g1, b1, out):
    nc = tc.nc
    x_tiles = x.rearrange("(i p) c h w -> i p (c h w)", p=P)
    w_tiles = w1.rearrange("(i p) k -> i p k", p=P)
    rows_in_dram = [x_tiles[i] for i in range(X_TILES)] + [w_tiles[j] for j in range(W_TILES)]
    out_tiles = out.rearrange("(t p) (j n) -> j p t n", p=P, n=P)

    with ExitStack() as ctx:
        const = ctx.enter_context(tc.tile_pool(name="const", bufs=1))
        raw_pool = ctx.enter_context(tc.tile_pool(name="raw", bufs=LOADS_AHEAD + 4))
        squares_pool = ctx.enter_context(tc.tile_pool(name="squares", bufs=2))
        unit_pool = ctx.enter_context(tc.tile_pool(name="unit", bufs=3))
        grouped_pool = ctx.enter_context(tc.tile_pool(name="grouped", bufs=4))
        weight_pool = ctx.enter_context(tc.tile_pool(name="weight", bufs=3))
        small = ctx.enter_context(tc.tile_pool(name="small", bufs=6))
        sim_pool = ctx.enter_context(tc.tile_pool(name="sim", bufs=6))
        normed_pool = ctx.enter_context(tc.tile_pool(name="normed", bufs=4))
        result_pool = ctx.enter_context(tc.tile_pool(name="result", bufs=8))
        turn_in_pool = ctx.enter_context(tc.psum_pool(name="turn_in", bufs=4))
        turn_out_pool = ctx.enter_context(tc.psum_pool(name="turn_out", bufs=2))
        acc_pool = ctx.enter_context(tc.psum_pool(name="acc", bufs=2))
        ctx.enter_context(tc.manual_schedule())

        one = const.tile([P, 1], F32)
        nc.vector.memset(one[:], 1.0)
        table_loaded = const.tile([P, 1], F32)
        nc.scalar.activation(out=table_loaded[:], in_=one[:], func=ACT.Sqrt)

        ident_f32 = const.tile([P, P], F32)
        nc.vector.memset(ident_f32[:], 0.0)
        masks.make_identity(nc, ident_f32[:], nomemset=True)

        x_codes = const.tile([P, PASSES, BATCH], U32, align_bytes=256)
        x_scales = const.tile([P, PASSES, BATCH], U8, align_bytes=256)

        raw, squared, norm, unit, turned_in, grouped = {}, {}, {}, {}, {}, {}
        weights, sums, sims, counts, fits, lines, normeds, turned_out = {}, {}, {}, {}, {}, {}, {}, {}

        vector_rows = const.tile([P, P], BF16)
        gain_shift = const.tile([P, 2 * W_TILES], F32)

        def load_gain_and_shift():
            nc.vector.memset(vector_rows[:], 0.0)
            nc.sync.dma_start(out=vector_rows[0:W_TILES, :], in_=g1.rearrange("(j n) -> j n", n=P))
            nc.sync.dma_start(
                out=vector_rows[W_TILES : 2 * W_TILES, :], in_=b1.rearrange("(j n) -> j n", n=P)
            )

        ident_bf16 = const.tile([P, P], BF16)
        turned_vectors = []

        def turn_gain_and_shift():
            vector_cols = turn_out_pool.tile([P, P], BF16, tag="turned_back")
            nc.tensor.transpose(vector_cols[:], vector_rows[:], ident_bf16[:])
            turned_vectors.append(vector_cols)

        def keep_gain_and_shift():
            vector_cols = turned_vectors[0]
            nc.vector.tensor_copy(out=gain_shift[:, 0:W_TILES], in_=vector_cols[:, 0:W_TILES])
            nc.vector.tensor_scalar_mul(
                out=gain_shift[:, W_TILES : 2 * W_TILES],
                in0=vector_cols[:, W_TILES : 2 * W_TILES],
                scalar1=-1.0,
            )

        def load(r):
            rows = raw_pool.tile([P, DEPTH], BF16)
            width = DEPTH // 2 if r < SPLIT_SQUARES else DEPTH
            for first in range(0, DEPTH, width):
                cols = slice(first, first + width)
                nc.sync.dma_start(out=rows[:, cols], in_=rows_in_dram[r][:, cols])
            raw[r] = rows

        def square(r):
            width = DEPTH // 2 if r < SPLIT_SQUARES else DEPTH
            squares = squares_pool.tile([P, DEPTH], BF16)
            sums_of_squares = small.tile([P, 1], F32)
            nc.scalar.activation(
                out=squares[:, 0:width], in_=raw[r][:, 0:width], func=ACT.Square,
                accum_out=sums_of_squares[:],
            )
            squared[r] = [sums_of_squares]
            if r < SPLIT_SQUARES:
                other_squares = squares_pool.tile([P, DEPTH // 2], BF16)
                other_sums = small.tile([P, 1], F32)
                nc.vector.scalar_tensor_tensor(
                    out=other_squares[:], in0=raw[r][:, width:], scalar=1.0, in1=raw[r][:, width:],
                    op0=ALU.mult, op1=ALU.mult, accum_out=other_sums[:],
                )
                squared[r].append(other_sums)

        def invert_first():
            lengths, padded, inverses = [], [], []
            for r in range(SPLIT_SQUARES):
                length = const.tile([P, 1], F32, name="length" + str(r))
                nc.scalar.activation(
                    out=length[:], in_=squared[r][0][:], func=ACT.Sqrt, bias=squared[r][1][:, 0:1]
                )
                lengths.append(length)
            for r in range(SPLIT_SQUARES):
                plus = const.tile([P, 1], F32, name="plus" + str(r))
                nc.vector.tensor_scalar(
                    out=plus[:], in0=lengths[r][:], scalar1=EPS, scalar2=1.0, op0=ALU.add, op1=ALU.mult
                )
                padded.append(plus)
            for r in range(SPLIT_SQUARES):
                inverse = const.tile([P, 1], F32, name="inverse" + str(r))
                nc.vector.reciprocal(out=inverse[:], in_=padded[r][:])
                norm[r] = inverse

        def take_length(r):
            length = small.tile([P, 1], F32)
            nc.scalar.activation(out=length[:], in_=squared[r][0][:], func=ACT.Sqrt)
            norm[r] = length

        def pad_length(r):
            padded = small.tile([P, 1], F32)
            nc.vector.tensor_scalar(
                out=padded[:], in0=norm[r][:], scalar1=EPS, scalar2=1.0, op0=ALU.add, op1=ALU.mult
            )
            norm[r] = padded

        def invert_length(r):
            inverse = small.tile([P, 1], F32)
            nc.vector.reciprocal(out=inverse[:], in_=norm[r][:])
            norm[r] = inverse

        def scale(place):
            r = ORDER[place]
            scaled = unit_pool.tile([P, DEPTH], BF16)
            if place < FIRST_REORDERED:
                nc.vector.tensor_scalar_mul(out=scaled[:], in0=raw[r][:], scalar1=norm[r][:, 0:1])
            else:
                nc.vector.tensor_scalar_mul(
                    out=scaled[:].rearrange("p (u w e) -> p u w e", u=2, e=2),
                    in0=raw[r][:].rearrange("p (w u e) -> p u w e", u=2, e=2),
                    scalar1=norm[r][:, 0:1],
                )
            unit[r] = scaled

        def turn(place):
            r = ORDER[place]
            pairs = unit[r][:].bitcast(F32)
            turned_in[r] = []
            for m in range(BANKS):
                turned = turn_in_pool.tile([P, PER_BANK, P], F32, tag="turned")
                for q in range(PER_BANK):
                    g, u = divmod(PER_BANK * m + q, 2)
                    if place < FIRST_REORDERED:
                        words = slice(2 * P * g + u, 2 * P * (g + 1), 2)
                    else:
                        words = slice((u * PASSES + g) * P, (u * PASSES + g + 1) * P)
                    nc.tensor.transpose(turned[:, q, :], pairs[:, words], ident_f32[:])
                turned_in[r].append(turned)

        def regroup(place, engine):
            r = ORDER[place]
            if r not in grouped:
                lined = grouped_pool.tile([P, DEPTH], BF16, align_bytes=256)
                grouped[r] = lined
            lined_pairs = grouped[r][:].bitcast(F32).rearrange("p (g c u) -> p g c u", g=PASSES, u=2)
            vector_banks = BANKS - scalar_banks(place)
            for m in range(vector_banks) if engine == "vector" else range(vector_banks, BANKS):
                source = turned_in[r][m][:].rearrange("p (g u) c -> p g c u", u=2)
                target = lined_pairs[:, 2 * m : 2 * m + 2, :, :]
                if engine == "vector":
                    nc.vector.tensor_copy(out=target, in_=source)
                else:
                    nc.scalar.copy(out=target, in_=source)

        def quantise(r):
            if r < X_TILES:
                cols = slice(r * P, (r + 1) * P)
                for g in range(PASSES):
                    nc.vector.quantize_mx(
                        out=x_codes[:, g, cols].bitcast(FP8X4),
                        scales=x_scales[:, g, cols],
                        in_=grouped[r][:, g * K_PASS : (g + 1) * K_PASS],
                    )
            else:
                w_codes = weight_pool.tile([P, PASSES * P], U32, align_bytes=256)
                w_scales = weight_pool.tile([P, PASSES * P], U8, align_bytes=256)
                for first, width in ((0, 4 * P), (4 * P, 2 * P)):
                    nc.vector.quantize_mx(
                        out=w_codes[:, first : first + width].bitcast(FP8X4),
                        scales=w_scales[:, first : first + width],
                        in_=grouped[r][:, PACK * first : PACK * (first + width)],
                    )
                weights[r - X_TILES] = (w_codes, w_scales)

        def multiply(j, first, width):
            w_codes, w_scales = weights[j]
            images = slice(first, first + width)
            acc = acc_pool.tile([P, N_MOVE], F32)
            for g in range(PASSES):
                w_cols = slice(g * P, (g + 1) * P)
                nc.tensor.matmul_mx(
                    out=acc[:, 0:width],
                    lhsT=w_codes[:, w_cols].bitcast(FP8X4),
                    lhsT_scale=w_scales[:, w_cols],
                    rhs=x_codes[:, g, images].bitcast(FP8X4),
                    rhs_scale=x_scales[:, g, images],
                    start=(g == 0),
                    stop=(g == PASSES - 1),
                )
            sums[j, first] = acc

        def clip(j, first, width):
            if j not in sims:
                sim = sim_pool.tile([P, BATCH], F32)
                sims[j] = sim
            nc.vector.tensor_scalar(
                out=sims[j][:, first : first + width], in0=sums[j, first][:, 0:width],
                scalar1=0.0, scalar2=1.0, op0=ALU.max, op1=ALU.min,
            )

        def count(j, first, width):
            parts = [part for part in chunks[j]]
            if j not in counts:
                stats = small.tile([P, len(parts), 6], F32, name="stats" + str(len(parts)))
                counts[j] = stats
            nc.vector.bn_stats(
                out=counts[j][:, parts.index((first, width)), :],
                in_=sims[j][:, first : first + width],
            )

        def fit(j):
            mean_var = small.tile([P, 2], F32)
            nc.vector.bn_aggr(out=mean_var[:], in_=counts[j][:].rearrange("p h s -> p (h s)"))
            fits[j] = mean_var

        def take_std(j):
            std = small.tile([P, 1], F32)
            nc.scalar.activation(out=std[:], in_=fits[j][:, 1:2], func=ACT.Sqrt, bias=BN_EPS)
            lines[j] = [std]

        def invert_std(j):
            inverse_std = small.tile([P, 1], F32)
            nc.vector.reciprocal(out=inverse_std[:], in_=lines[j][0][:])
            lines[j] = [inverse_std]

        def make_slope(j):
            slope = small.tile([P, 1], F32)
            nc.vector.tensor_scalar_mul(
                out=slope[:], in0=lines[j][0][:], scalar1=gain_shift[:, j : j + 1]
            )
            lines[j] = [slope]

        def make_drop(j):
            drop = small.tile([P, 1], F32)
            nc.vector.tensor_scalar(
                out=drop[:], in0=fits[j][:, 0:1], scalar1=lines[j][0][:, 0:1],
                scalar2=gain_shift[:, W_TILES + j : W_TILES + j + 1],
                op0=ALU.mult, op1=ALU.add,
            )
            lines[j].append(drop)

        def normalise(j):
            slope, drop = lines[j]
            normed = normed_pool.tile([P, BATCH], F32)
            for h in range(HALVES):
                half_cols = slice(h * N_MOVE, (h + 1) * N_MOVE)
                nc.vector.tensor_scalar(
                    out=normed[:, half_cols], in0=sims[j][:, half_cols],
                    scalar1=slope[:, 0:1], scalar2=drop[:, 0:1],
                    op0=ALU.mult, op1=ALU.subtract,
                )
            normeds[j] = normed

        def turn_back(j):
            turned_out[j] = []
            for m in range(X_TILES // PER_BANK):
                if m > 0 and j >= FIRST_SPREAD:
                    turned_back = turn_in_pool.tile([P, PER_BANK, P], F32, tag="turned")
                else:
                    turned_back = turn_out_pool.tile([P, PER_BANK, P], F32, tag="turned_back")
                for q in range(PER_BANK):
                    t = PER_BANK * m + q
                    nc.tensor.transpose(
                        turned_back[:, q, :], normeds[j][:, t * P : (t + 1) * P], ident_f32[:]
                    )
                turned_out[j].append(turned_back)

        def store(j):
            for m in range(X_TILES // PER_BANK):
                result = result_pool.tile([P, PER_BANK, P], F32)
                if m == 1 and j == W_TILES - 1:
                    nc.vector.tensor_copy(out=result[:], in_=turned_out[j][m][:])
                else:
                    nc.scalar.copy(out=result[:], in_=turned_out[j][m][:])
                nc.sync.dma_start(
                    out=out_tiles[j][:, PER_BANK * m : PER_BANK * (m + 1), :], in_=result[:]
                )

        place_of = {ORDER[place]: place for place in range(ROW_TILES)}
        chunks, matmuls, fitted_in = {}, {}, {}
        for j in range(W_TILES):
            early = place_of[X_TILES + j] < place_of[X_TILES - 1]
            quarter = N_MOVE // 2
            chunks[j] = [(0, N_MOVE)]
            chunks[j] += [(N_MOVE, quarter), (N_MOVE + quarter, quarter)] if early else [(N_MOVE, N_MOVE)]
        for j in range(W_TILES):
            for first, width in chunks[j]:
                needed = [place_of[i] for i in range(first // P, (first + width) // P)]
                step = max(needed + [place_of[X_TILES + j]]) + MATMUL_LAG
                matmuls.setdefault(step, []).append((j, first, width))
        for step in matmuls:
            for n, part in enumerate(matmuls[step]):
                fitted_in[part[0]] = max(fitted_in.get(part[0], 0), step + 1 + n)

        def tiles_at(step, lag):
            return [j for j in range(W_TILES) if fitted_in[j] + lag == step]

        for place in range(LOADS_AHEAD):
            load(ORDER[place])
        load_gain_and_shift()
        for r in range(SPLIT_SQUARES):
            square(r)
        invert_first()
        for step in range(1, max(fitted_in.values()) + LINE_LAG + 1):
            now = matmuls.get(step, [])
            before = matmuls.get(step - 1, [])
            for part in before[1:]:
                clip(*part)
            if step - 1 < ROW_TILES:
                scale(step - 1)
            for j in tiles_at(step, 1):
                invert_std(j)
            if 0 <= step - 2 < ROW_TILES:
                regroup(step - 2, "vector")
            for j in tiles_at(step, 0):
                fit(j)
            if SPLIT_SQUARES <= step < ROW_TILES:
                pad_length(ORDER[step])
            for j in tiles_at(step, LINE_LAG):
                normalise(j)
            for j in tiles_at(step, 1):
                make_slope(j)
            for part in now:
                multiply(*part)
            for j in tiles_at(step, LINE_LAG):
                turn_back(j)
            if step - 1 < ROW_TILES:
                turn(step - 1)
            if step + 1 < ROW_TILES:
                square(ORDER[step + 1])
            if step - 1 < ROW_TILES:
                regroup(step - 1, "scalar")
            if step + 1 < ROW_TILES:
                take_length(ORDER[step + 1])
            for j in tiles_at(step, 0):
                take_std(j)
            for j in tiles_at(step, LINE_LAG):
                store(j)
            for part in now[:1]:
                clip(*part)
            for part in before[1:]:
                count(*part)
            if 0 <= step - 2 < ROW_TILES:
                quantise(ORDER[step - 2])
            if SPLIT_SQUARES <= step < ROW_TILES:
                invert_length(ORDER[step])
            for j in tiles_at(step, 1):
                make_drop(j)
            for part in now[:1]:
                count(*part)
            if step - 1 + LOADS_AHEAD < ROW_TILES:
                load(ORDER[step - 1 + LOADS_AHEAD])
            if step == 2:
                nc.gpsimd.tensor_copy(out=ident_bf16[:], in_=ident_f32[:])
            if step == 3:
                turn_gain_and_shift()
            if step == 4:
                keep_gain_and_shift()
